import numpy as np
import ml_dtypes


def mxq(x, axis, fmt="e4m3"):
    dtype, down = {"e4m3": (ml_dtypes.float8_e4m3fn, 7), "e5m2": (ml_dtypes.float8_e5m2, 14)}[fmt]
    v = np.moveaxis(np.asarray(x, np.float32).astype(ml_dtypes.bfloat16).astype(np.float64), axis, -1)
    blocks = v.reshape(v.shape[:-1] + (-1, 32))
    amax = np.abs(blocks).max(-1, keepdims=True)
    byte = np.maximum(np.where(amax > 0, np.frexp(amax)[1] - 1 + 127, 0) - down, 1)
    scale = np.exp2(byte - 127.0)
    codes = (blocks / scale).astype(np.float32).astype(dtype).astype(np.float64)
    return np.moveaxis((codes * scale).reshape(v.shape), -1, axis)


WIDE = False


def mx_kscale(k):
    if not WIDE:
        return np.ones(k)
    levels = np.array([10, -10, 5, -5, 0])
    a = np.random.permutation(np.resize(levels, k // 512 * 4)).reshape(k // 512, 4)
    idx = np.arange(k)
    return np.exp2(a[idx // 512, idx % 128 // 32])


BF16 = ml_dtypes.bfloat16


def bf(x):
    return np.asarray(x, np.float32).astype(BF16)


def f64(x):
    return np.asarray(x).astype(np.float64)


E2M1 = np.array([0.0, 0.5, 1.0, 1.5, 2.0, 3.0, 4.0, 6.0, -0.0, -0.5, -1.0, -1.5, -2.0, -3.0, -4.0, -6.0])


def pack_weight(w, fmt):
    k, n = w.shape
    w = f64(bf(w)).reshape(k // 32, 32, n)
    amax = np.abs(w).max(1)
    if fmt == "e4m3":
        byte = np.frexp(amax)[1] - 1 + 127 - 7
    else:
        mant, ex = np.frexp(amax / 6.0)
        byte = np.where(mant > 0.5, ex, ex - 1) + 127
    byte = np.clip(np.where(amax > 0, byte, 1), 1, 254)
    scaled = (w * np.exp2(127.0 - byte)[:, None, :]).reshape(k, n).astype(np.float32)
    by_word = np.ascontiguousarray(scaled.reshape(k // 512, 128, 4, n).transpose(0, 1, 3, 2))
    if fmt == "e4m3":
        words = by_word.astype(ml_dtypes.float8_e4m3fn).view(np.uint8)
    else:
        c = by_word.astype(ml_dtypes.float4_e2m1fn).view(np.uint8) & 0xF
        words = c[..., 0::2] | (c[..., 1::2] << 4)
    return np.ascontiguousarray(words), np.ascontiguousarray(byte.astype(np.uint8).reshape(k // 512, 16, n))


def unpack_weight(words, scales, fmt):
    g, p, n, _ = words.shape
    if fmt == "e4m3":
        vals = np.ascontiguousarray(words).view(ml_dtypes.float8_e4m3fn).astype(np.float64)
    else:
        nib = np.empty((g, p, n, 4), np.uint8)
        nib[..., 0::2] = words & 0xF
        nib[..., 1::2] = words >> 4
        vals = E2M1[nib]
    vals = vals * np.repeat(np.exp2(scales.astype(np.float64) - 127.0), 8, axis=1)[..., None]
    return vals.transpose(0, 1, 3, 2).reshape(g * 512, n)


B, S, D, H, DH, QB = 1, 256, 8192, 8, 128, 512
HD = H * DH
ROPE_BASE = 10000.0
FMT = "e4m3"


def rope(t):
    b, h, s, d = t.shape
    inv_freq = 1.0 / (ROPE_BASE ** (np.arange(0, d, 2) / d))
    ang = np.arange(s)[:, None] * inv_freq[None, :]
    cos = np.cos(ang)[None, None]
    sin = np.sin(ang)[None, None]
    t1 = t[..., 0::2]
    t2 = t[..., 1::2]
    r1 = t1 * cos - t2 * sin
    r2 = t1 * sin + t2 * cos
    return np.stack([r1, r2], axis=-1).reshape(b, h, s, d)


def setup_inputs():
    s = mx_kscale(D)
    x = bf(np.random.standard_normal((B, S, D)) * s)
    wq = np.random.standard_normal((HD, D)) / np.sqrt(D) / s[None, :]
    wk = np.random.standard_normal((HD, D)) / np.sqrt(D) / s[None, :]
    wq_words, wq_scales = pack_weight(wq.T, FMT)
    wk_words, wk_scales = pack_weight(wk.T, FMT)
    return {"x": x,
            "wq_words": wq_words, "wq_scales": wq_scales,
            "wk_words": wk_words, "wk_scales": wk_scales}


def reference(x, wq_words, wq_scales, wk_words, wk_scales):
    xq = mxq(f64(x), 2, "e4m3")
    q = (xq @ unpack_weight(wq_words, wq_scales, FMT)).reshape(B, S, H, DH).transpose(0, 2, 1, 3)
    k = (xq @ unpack_weight(wk_words, wk_scales, FMT)).reshape(B, S, H, DH).transpose(0, 2, 1, 3)
    return np.maximum(rope(q), 0.0), np.maximum(rope(k), 0.0)

@@ -1,0 +1,270 @@
+import math
+from contextlib import ExitStack
+
+import concourse.masks as masks
+import concourse.mybir as mybir
+
+F32 = mybir.dt.float32
+BF16 = mybir.dt.bfloat16
+I32 = mybir.dt.int32
+U32 = mybir.dt.uint32
+U8 = mybir.dt.uint8
+FP8X4 = mybir.dt.float8_e4m3fn_x4
+ALU = mybir.AluOpType
+ACT = mybir.ActivationFunctionType
+
+P = 128
+PACK = 4
+K_PASS = P * PACK
+TOKENS = 256
+TOKEN_TILES = TOKENS // P
+D_MODEL = 8192
+GROUPS = D_MODEL // K_PASS
+N_WEIGHT = 1024
+N_BLOCK = 512
+HEAD_DIM = 128
+PAIRS = HEAD_DIM // 2
+HEADS_PER_BLOCK = N_BLOCK // HEAD_DIM
+ROPE_BASE = 10000.0
+
+X_GROUPS = 4
+UNIT_GROUPS = 2
+W_GROUPS = 2
+PLANES_PER_TILE = 4
+SCALE_LOADS_PER_BIG_LOAD = 2
+
+ROUND_MAGIC = 12582912.0
+
+FLOPS = 2 * TOKENS * D_MODEL * 2 * N_WEIGHT
+
+
+def tile_linearattention_pa_k_kernel(
+    tc, x, wq_words, wq_scales, wk_words, wk_scales, out_0, out_1
+):
+    nc = tc.nc
+    weights = [(wq_words, wq_scales, out_0), (wk_words, wk_scales, out_1)]
+    blocks = [(w, n0) for w in range(len(weights)) for n0 in range(0, N_WEIGHT, N_BLOCK)]
+
+    with ExitStack() as ctx:
+        keep = ctx.enter_context(tc.tile_pool(name="keep", bufs=1))
+        stage = ctx.enter_context(tc.tile_pool(name="stage", bufs=3))
+        rope = ctx.enter_context(tc.tile_pool(name="rope", bufs=2))
+        psum = ctx.enter_context(tc.psum_pool(name="psum", bufs=8))
+
+        planes = keep.tile(
+            [P, len(weights), GROUPS // PLANES_PER_TILE, N_WEIGHT], U8, align_bytes=64
+        )
+        nc.vector.memset(planes[:].bitcast(I32), 0)
+
+        scale_loads = [
+            (w, a, quadrant)
+            for w in range(len(weights))
+            for a in range(GROUPS // PLANES_PER_TILE)
+            for quadrant in range(4)
+        ]
+
+        def load_scales(w, a, quadrant):
+            nc.sync.dma_start(
+                out=planes[32 * quadrant : 32 * quadrant + 16, w, a, :].bitcast(I32),
+                in_=weights[w][1][
+                    PLANES_PER_TILE * a : PLANES_PER_TILE * (a + 1),
+                    4 * quadrant : 4 * quadrant + 4,
+                    :,
+                ].bitcast(I32),
+            )
+
+        def load_x(i, piece):
+            x_sb = keep.tile([P, X_GROUPS * K_PASS], BF16, name="x_%d_%d" % (i, piece))
+            first = piece * X_GROUPS * K_PASS
+            nc.sync.dma_start(
+                out=x_sb[:], in_=x[0, i * P : (i + 1) * P, first : first + X_GROUPS * K_PASS]
+            )
+            return x_sb
+
+        def load_words(w, n0, g0):
+            w_sb = keep.tile(
+                [P, W_GROUPS, N_BLOCK], U32, name="w_%d_%d_%d" % (w, n0, g0), align_bytes=64
+            )
+            nc.sync.dma_start(
+                out=w_sb[:].bitcast(I32),
+                in_=weights[w][0][g0 : g0 + W_GROUPS, :, n0 : n0 + N_BLOCK, :]
+                .rearrange("g p n t -> p g (n t)")
+                .bitcast(I32),
+            )
+            return w_sb
+
+        def load_scales_behind(big_load):
+            first = SCALE_LOADS_PER_BIG_LOAD * big_load
+            for w, a, quadrant in scale_loads[first : first + SCALE_LOADS_PER_BIG_LOAD]:
+                load_scales(w, a, quadrant)
+
+        big_loads = 0
+        x_tiles = {}
+        for piece in range(GROUPS // X_GROUPS):
+            for i in range(TOKEN_TILES):
+                x_tiles[(i, piece)] = load_x(i, piece)
+                load_scales_behind(big_loads)
+                big_loads += 1
+        w_tiles = {}
+        for w, n0 in blocks:
+            for g0 in range(0, GROUPS, W_GROUPS):
+                w_tiles[(w, n0, g0)] = load_words(w, n0, g0)
+                load_scales_behind(big_loads)
+                big_loads += 1
+
+        identity = keep.tile([P, P], F32)
+        masks.make_identity(nc, identity[:])
+        position_int = keep.tile([P, TOKEN_TILES], I32)
+        nc.gpsimd.iota(position_int[:], pattern=[[P, TOKEN_TILES]], base=0, channel_multiplier=1)
+        position = keep.tile([P, TOKEN_TILES], F32)
+        nc.vector.tensor_scalar(
+            out=position[:],
+            in0=position_int[:],
+            scalar1=1.0 / (2.0 * math.pi),
+            scalar2=None,
+            op0=ALU.mult,
+        )
+
+        frequency = keep.tile([P, PAIRS], F32)
+        nc.vector.memset(frequency[:, 0:1], 1.0)
+        width = 1
+        while width < PAIRS:
+            nc.vector.tensor_scalar(
+                out=frequency[:, width : 2 * width],
+                in0=frequency[:, 0:width],
+                scalar1=ROPE_BASE ** (-width / PAIRS),
+                scalar2=None,
+                op0=ALU.mult,
+            )
+            width *= 2
+
+        turns = keep.tile([P, TOKEN_TILES, 2, PAIRS], F32)
+        for i in range(TOKEN_TILES):
+            for quarter in range(2):
+                nc.vector.tensor_scalar(
+                    out=turns[:, i, quarter, :],
+                    in0=frequency[:],
+                    scalar1=position[:, i : i + 1],
+                    scalar2=0.25 * quarter,
+                    op0=ALU.mult,
+                    op1=ALU.add,
+                )
+        whole_turns = keep.tile([P, TOKEN_TILES, 2, PAIRS], F32)
+        nc.vector.tensor_scalar(
+            out=whole_turns[:],
+            in0=turns[:],
+            scalar1=ROUND_MAGIC,
+            scalar2=ROUND_MAGIC,
+            op0=ALU.add,
+            op1=ALU.subtract,
+        )
+        part_turns = keep.tile([P, TOKEN_TILES, 2, PAIRS], F32)
+        nc.vector.tensor_tensor(
+            out=part_turns[:], in0=turns[:], in1=whole_turns[:], op=ALU.subtract
+        )
+
+        even_coef = keep.tile([P, TOKEN_TILES, PAIRS, 2], F32)
+        odd_coef = keep.tile([P, TOKEN_TILES, PAIRS, 2], F32)
+        for coef, slot, quarter, sign in (
+            (even_coef, 0, 1, 1.0),
+            (even_coef, 1, 0, 1.0),
+            (odd_coef, 0, 0, -1.0),
+            (odd_coef, 1, 1, 1.0),
+        ):
+            nc.scalar.activation(
+                out=coef[:, :, :, slot],
+                in_=part_turns[:, :, quarter, :],
+                func=ACT.Sin,
+                scale=sign * 2.0 * math.pi,
+            )
+
+        x_codes = keep.tile([P, TOKEN_TILES, GROUPS, P], U32, align_bytes=64)
+        x_scales = keep.tile([P, TOKEN_TILES, GROUPS, P], U8, align_bytes=64)
+
+        def regroup(i, g0, copy_engine):
+            x_words = x_tiles[(i, g0 // X_GROUPS)][:].bitcast(F32)
+            halves = psum.tile([P, UNIT_GROUPS, 2, P], F32, tag="bank", name="halves")
+            for gg in range(UNIT_GROUPS):
+                first = (K_PASS // 2) * ((g0 + gg) % X_GROUPS)
+                for u in range(2):
+                    nc.tensor.transpose(
+                        halves[:, gg, u, :],
+                        x_words[:, first + u : first + K_PASS // 2 : 2],
+                        identity[:],
+                    )
+            grouped = stage.tile([P, UNIT_GROUPS, P, PACK], BF16, align_bytes=64, name="grouped")
+            copy_engine(
+                out=grouped[:].bitcast(F32), in_=halves[:].rearrange("p g u s -> p g s u")
+            )
+            return grouped
+
+        def quantise(i, g0, grouped):
+            nc.vector.quantize_mx(
+                out=x_codes[:, i, g0 : g0 + UNIT_GROUPS, :]
+                .rearrange("p g s -> p (g s)")
+                .bitcast(FP8X4),
+                scales=x_scales[:, i, g0 : g0 + UNIT_GROUPS, :].rearrange("p g s -> p (g s)"),
+                in_=grouped[:].rearrange("p g s t -> p (g s t)"),
+            )
+
+        waiting = None
+        for g0 in range(0, GROUPS, UNIT_GROUPS):
+            for i in range(TOKEN_TILES):
+                copy_engine = nc.vector.tensor_copy if i == 0 else nc.scalar.copy
+                grouped = regroup(i, g0, copy_engine)
+                if waiting is not None:
+                    quantise(*waiting)
+                waiting = (i, g0, grouped)
+        quantise(*waiting)
+
+        pair_shape = [P, HEADS_PER_BLOCK, PAIRS, 2]
+
+        def rope_relu_store(acc, i, out, n0):
+            pairs = acc[:].rearrange("p (h j e) -> p h j e", h=HEADS_PER_BLOCK, e=2)
+            from_even = rope.tile(pair_shape, F32, name="from_even")
+            nc.vector.tensor_tensor(
+                out=from_even[:],
+                in0=pairs[:, :, :, 0:1].to_broadcast(pair_shape),
+                in1=even_coef[:, i, :, :].unsqueeze(1).to_broadcast(pair_shape),
+                op=ALU.mult,
+            )
+            from_odd = rope.tile(pair_shape, F32, name="from_odd")
+            nc.vector.tensor_tensor(
+                out=from_odd[:],
+                in0=pairs[:, :, :, 1:2].to_broadcast(pair_shape),
+                in1=odd_coef[:, i, :, :].unsqueeze(1).to_broadcast(pair_shape),
+                op=ALU.mult,
+            )
+            nc.vector.tensor_tensor(
+                out=from_even[:], in0=from_even[:], in1=from_odd[:], op=ALU.add
+            )
+            result = rope.tile(pair_shape, F32, name="result")
+            nc.scalar.activation(out=result[:], in_=from_even[:], func=ACT.Relu)
+            h0 = n0 // HEAD_DIM
+            nc.scalar.dma_start(
+                out=out[0, h0 : h0 + HEADS_PER_BLOCK, i * P : (i + 1) * P, :].rearrange(
+                    "h s d -> s h d"
+                ),
+                in_=result[:].rearrange("p h j e -> p h (j e)"),
+            )
+
+        for w, n0 in blocks:
+            accs = [
+                psum.tile([P, N_BLOCK], F32, tag="bank", name="acc_%d" % i)
+                for i in range(TOKEN_TILES)
+            ]
+            for g in range(GROUPS):
+                w_sb = w_tiles[(w, n0, g - g % W_GROUPS)]
+                a, b = divmod(g, PLANES_PER_TILE)
+                for i in range(TOKEN_TILES):
+                    nc.tensor.matmul_mx(
+                        out=accs[i][:],
+                        lhsT=x_codes[:, i, g, :].bitcast(FP8X4),
+                        lhsT_scale=x_scales[:, i, g, :],
+                        rhs=w_sb[:, g % W_GROUPS, :].bitcast(FP8X4),
+                        rhs_scale=planes[4 * b : P, w, a, n0 : n0 + N_BLOCK],
+                        start=(g == 0),
+                        stop=(g == GROUPS - 1),
+                    )
+            for i in range(TOKEN_TILES):
+                rope_relu_store(accs[i], i, weights[w][2], n0)

@@ -49,6 +49,7 @@ def tile_linearattention_pa_k_kernel(
         keep = ctx.enter_context(tc.tile_pool(name="keep", bufs=1))
         stage = ctx.enter_context(tc.tile_pool(name="stage", bufs=3))
         rope = ctx.enter_context(tc.tile_pool(name="rope", bufs=2))
+        results = ctx.enter_context(tc.tile_pool(name="results", bufs=1))
         psum = ctx.enter_context(tc.psum_pool(name="psum", bufs=8))
 
         planes = keep.tile(
@@ -219,7 +220,8 @@ def tile_linearattention_pa_k_kernel(
 
         pair_shape = [P, HEADS_PER_BLOCK, PAIRS, 2]
 
-        def rope_relu_store(acc, i, out, n0):
+        def rope_relu_store(acc, i, w, n0):
+            out = weights[w][2]
             pairs = acc[:].rearrange("p (h j e) -> p h j e", h=HEADS_PER_BLOCK, e=2)
             from_even = rope.tile(pair_shape, F32, name="from_even")
             nc.vector.tensor_tensor(
@@ -238,10 +240,10 @@ def tile_linearattention_pa_k_kernel(
             nc.vector.tensor_tensor(
                 out=from_even[:], in0=from_even[:], in1=from_odd[:], op=ALU.add
             )
-            result = rope.tile(pair_shape, F32, name="result")
+            result = results.tile(pair_shape, F32, name="result_%d_%d_%d" % (w, n0, i))
             nc.scalar.activation(out=result[:], in_=from_even[:], func=ACT.Relu)
             h0 = n0 // HEAD_DIM
-            nc.scalar.dma_start(
+            nc.sync.dma_start(
                 out=out[0, h0 : h0 + HEADS_PER_BLOCK, i * P : (i + 1) * P, :].rearrange(
                     "h s d -> s h d"
                 ),
@@ -253,18 +255,19 @@ def tile_linearattention_pa_k_kernel(
                 psum.tile([P, N_BLOCK], F32, tag="bank", name="acc_%d" % i)
                 for i in range(TOKEN_TILES)
             ]
-            for g in range(GROUPS):
-                w_sb = w_tiles[(w, n0, g - g % W_GROUPS)]
-                a, b = divmod(g, PLANES_PER_TILE)
+            for g0 in range(0, GROUPS, W_GROUPS):
+                w_sb = w_tiles[(w, n0, g0)]
                 for i in range(TOKEN_TILES):
-                    nc.tensor.matmul_mx(
-                        out=accs[i][:],
-                        lhsT=x_codes[:, i, g, :].bitcast(FP8X4),
-                        lhsT_scale=x_scales[:, i, g, :],
-                        rhs=w_sb[:, g % W_GROUPS, :].bitcast(FP8X4),
-                        rhs_scale=planes[4 * b : P, w, a, n0 : n0 + N_BLOCK],
-                        start=(g == 0),
-                        stop=(g == GROUPS - 1),
-                    )
+                    for g in range(g0, g0 + W_GROUPS):
+                        a, b = divmod(g, PLANES_PER_TILE)
+                        nc.tensor.matmul_mx(
+                            out=accs[i][:],
+                            lhsT=x_codes[:, i, g, :].bitcast(FP8X4),
+                            lhsT_scale=x_scales[:, i, g, :],
+                            rhs=w_sb[:, g - g0, :].bitcast(FP8X4),
+                            rhs_scale=planes[4 * b : P, w, a, n0 : n0 + N_BLOCK],
+                            start=(g == 0),
+                            stop=(g == GROUPS - 1),
+                        )
             for i in range(TOKEN_TILES):
-                rope_relu_store(accs[i], i, weights[w][2], n0)
+                rope_relu_store(accs[i], i, w, n0)

@@ -31,7 +31,6 @@ X_GROUPS = 4
 UNIT_GROUPS = 2
 W_GROUPS = 2
 PLANES_PER_TILE = 4
-SCALE_LOADS_PER_BIG_LOAD = 2
 
 ROUND_MAGIC = 12582912.0
 
@@ -57,22 +56,22 @@ def tile_linearattention_pa_k_kernel(
         )
         nc.vector.memset(planes[:].bitcast(I32), 0)
 
-        scale_loads = [
-            (w, a, quadrant)
-            for w in range(len(weights))
-            for a in range(GROUPS // PLANES_PER_TILE)
-            for quadrant in range(4)
-        ]
+        identity = keep.tile([P, P], F32)
+        masks.make_identity(nc, identity[:])
+        position_int = keep.tile([P, TOKEN_TILES], I32)
+        nc.gpsimd.iota(position_int[:], pattern=[[P, TOKEN_TILES]], base=0, channel_multiplier=1)
 
-        def load_scales(w, a, quadrant):
-            nc.sync.dma_start(
-                out=planes[32 * quadrant : 32 * quadrant + 16, w, a, :].bitcast(I32),
-                in_=weights[w][1][
-                    PLANES_PER_TILE * a : PLANES_PER_TILE * (a + 1),
-                    4 * quadrant : 4 * quadrant + 4,
-                    :,
-                ].bitcast(I32),
-            )
+        for w in range(len(weights)):
+            for a in range(GROUPS // PLANES_PER_TILE):
+                for quadrant in range(4):
+                    nc.gpsimd.dma_start(
+                        out=planes[32 * quadrant : 32 * quadrant + 16, w, a, :].bitcast(F32),
+                        in_=weights[w][1][
+                            PLANES_PER_TILE * a : PLANES_PER_TILE * (a + 1),
+                            4 * quadrant : 4 * quadrant + 4,
+                            :,
+                        ].bitcast(F32),
+                    )
 
         def load_x(i, piece):
             x_sb = keep.tile([P, X_GROUPS * K_PASS], BF16, name="x_%d_%d" % (i, piece))
@@ -94,29 +93,15 @@ def tile_linearattention_pa_k_kernel(
             )
             return w_sb
 
-        def load_scales_behind(big_load):
-            first = SCALE_LOADS_PER_BIG_LOAD * big_load
-            for w, a, quadrant in scale_loads[first : first + SCALE_LOADS_PER_BIG_LOAD]:
-                load_scales(w, a, quadrant)
-
-        big_loads = 0
         x_tiles = {}
         for piece in range(GROUPS // X_GROUPS):
             for i in range(TOKEN_TILES):
                 x_tiles[(i, piece)] = load_x(i, piece)
-                load_scales_behind(big_loads)
-                big_loads += 1
         w_tiles = {}
         for w, n0 in blocks:
             for g0 in range(0, GROUPS, W_GROUPS):
                 w_tiles[(w, n0, g0)] = load_words(w, n0, g0)
-                load_scales_behind(big_loads)
-                big_loads += 1
 
-        identity = keep.tile([P, P], F32)
-        masks.make_identity(nc, identity[:])
-        position_int = keep.tile([P, TOKEN_TILES], I32)
-        nc.gpsimd.iota(position_int[:], pattern=[[P, TOKEN_TILES]], base=0, channel_multiplier=1)
         position = keep.tile([P, TOKEN_TILES], F32)
         nc.vector.tensor_scalar(
             out=position[:],

@@ -27,9 +27,9 @@ PAIRS = HEAD_DIM // 2
 HEADS_PER_BLOCK = N_BLOCK // HEAD_DIM
 ROPE_BASE = 10000.0
 
-X_GROUPS = 4
+X_GROUPS = 8
 UNIT_GROUPS = 2
-W_GROUPS = 2
+W_LOAD_WORDS = 1024
 PLANES_PER_TILE = 4
 
 ROUND_MAGIC = 12582912.0
@@ -42,7 +42,7 @@ def tile_linearattention_pa_k_kernel(
 ):
     nc = tc.nc
     weights = [(wq_words, wq_scales, out_0), (wk_words, wk_scales, out_1)]
-    blocks = [(w, n0) for w in range(len(weights)) for n0 in range(0, N_WEIGHT, N_BLOCK)]
+    blocks = [(0, 0, N_WEIGHT), (1, 0, N_BLOCK), (1, N_BLOCK, N_BLOCK)]
 
     with ExitStack() as ctx:
         keep = ctx.enter_context(tc.tile_pool(name="keep", bufs=1))
@@ -59,7 +59,9 @@ def tile_linearattention_pa_k_kernel(
         identity = keep.tile([P, P], F32)
         masks.make_identity(nc, identity[:])
         position_int = keep.tile([P, TOKEN_TILES], I32)
-        nc.gpsimd.iota(position_int[:], pattern=[[P, TOKEN_TILES]], base=0, channel_multiplier=1)
+        nc.gpsimd.iota(
+            position_int[:], pattern=[[1, TOKEN_TILES]], base=0, channel_multiplier=TOKEN_TILES
+        )
 
         for w in range(len(weights)):
             for a in range(GROUPS // PLANES_PER_TILE):
@@ -73,21 +75,22 @@ def tile_linearattention_pa_k_kernel(
                         ].bitcast(F32),
                     )
 
+        x_by_tile = x[0].rearrange("(p i) k -> p i k", i=TOKEN_TILES)
+
         def load_x(i, piece):
             x_sb = keep.tile([P, X_GROUPS * K_PASS], BF16, name="x_%d_%d" % (i, piece))
             first = piece * X_GROUPS * K_PASS
-            nc.sync.dma_start(
-                out=x_sb[:], in_=x[0, i * P : (i + 1) * P, first : first + X_GROUPS * K_PASS]
-            )
+            nc.sync.dma_start(out=x_sb[:], in_=x_by_tile[:, i, first : first + X_GROUPS * K_PASS])
             return x_sb
 
-        def load_words(w, n0, g0):
+        def load_words(w, n0, width, g0):
+            groups = W_LOAD_WORDS // width
             w_sb = keep.tile(
-                [P, W_GROUPS, N_BLOCK], U32, name="w_%d_%d_%d" % (w, n0, g0), align_bytes=64
+                [P, groups, width], U32, name="w_%d_%d_%d" % (w, n0, g0), align_bytes=64
             )
             nc.sync.dma_start(
                 out=w_sb[:].bitcast(I32),
-                in_=weights[w][0][g0 : g0 + W_GROUPS, :, n0 : n0 + N_BLOCK, :]
+                in_=weights[w][0][g0 : g0 + groups, :, n0 : n0 + width, :]
                 .rearrange("g p n t -> p g (n t)")
                 .bitcast(I32),
             )
@@ -98,9 +101,9 @@ def tile_linearattention_pa_k_kernel(
             for i in range(TOKEN_TILES):
                 x_tiles[(i, piece)] = load_x(i, piece)
         w_tiles = {}
-        for w, n0 in blocks:
-            for g0 in range(0, GROUPS, W_GROUPS):
-                w_tiles[(w, n0, g0)] = load_words(w, n0, g0)
+        for w, n0, width in blocks:
+            for g0 in range(0, GROUPS, W_LOAD_WORDS // width):
+                w_tiles[(w, n0, g0)] = load_words(w, n0, width, g0)
 
         position = keep.tile([P, TOKEN_TILES], F32)
         nc.vector.tensor_scalar(
@@ -205,54 +208,71 @@ def tile_linearattention_pa_k_kernel(
 
         pair_shape = [P, HEADS_PER_BLOCK, PAIRS, 2]
 
-        def rope_relu_store(acc, i, w, n0):
-            out = weights[w][2]
-            pairs = acc[:].rearrange("p (h j e) -> p h j e", h=HEADS_PER_BLOCK, e=2)
-            from_even = rope.tile(pair_shape, F32, name="from_even")
-            nc.vector.tensor_tensor(
-                out=from_even[:],
-                in0=pairs[:, :, :, 0:1].to_broadcast(pair_shape),
-                in1=even_coef[:, i, :, :].unsqueeze(1).to_broadcast(pair_shape),
-                op=ALU.mult,
-            )
-            from_odd = rope.tile(pair_shape, F32, name="from_odd")
-            nc.vector.tensor_tensor(
-                out=from_odd[:],
-                in0=pairs[:, :, :, 1:2].to_broadcast(pair_shape),
-                in1=odd_coef[:, i, :, :].unsqueeze(1).to_broadcast(pair_shape),
-                op=ALU.mult,
-            )
-            nc.vector.tensor_tensor(
-                out=from_even[:], in0=from_even[:], in1=from_odd[:], op=ALU.add
-            )
-            result = results.tile(pair_shape, F32, name="result_%d_%d_%d" % (w, n0, i))
-            nc.scalar.activation(out=result[:], in_=from_even[:], func=ACT.Relu)
-            h0 = n0 // HEAD_DIM
-            nc.sync.dma_start(
-                out=out[0, h0 : h0 + HEADS_PER_BLOCK, i * P : (i + 1) * P, :].rearrange(
-                    "h s d -> s h d"
-                ),
-                in_=result[:].rearrange("p h j e -> p h (j e)"),
-            )
+        def rope_relu(banks, result):
+            products = []
+            for i in range(TOKEN_TILES):
+                pairs = banks[i][:].rearrange("p (h j e) -> p h j e", h=HEADS_PER_BLOCK, e=2)
+                from_even = rope.tile(pair_shape, F32, name="from_even")
+                nc.vector.tensor_tensor(
+                    out=from_even[:],
+                    in0=pairs[:, :, :, 0:1].to_broadcast(pair_shape),
+                    in1=even_coef[:, i, :, :].unsqueeze(1).to_broadcast(pair_shape),
+                    op=ALU.mult,
+                )
+                from_odd = rope.tile(pair_shape, F32, name="from_odd")
+                nc.vector.tensor_tensor(
+                    out=from_odd[:],
+                    in0=pairs[:, :, :, 1:2].to_broadcast(pair_shape),
+                    in1=odd_coef[:, i, :, :].unsqueeze(1).to_broadcast(pair_shape),
+                    op=ALU.mult,
+                )
+                products.append((from_even, from_odd))
+            for i in range(TOKEN_TILES):
+                from_even, from_odd = products[i]
+                nc.vector.tensor_tensor(
+                    out=from_even[:], in0=from_even[:], in1=from_odd[:], op=ALU.add
+                )
+                nc.scalar.activation(
+                    out=result[:, :, i, :],
+                    in_=from_even[:].rearrange("p h j e -> p h (j e)"),
+                    func=ACT.Relu,
+                )
 
-        for w, n0 in blocks:
-            accs = [
-                psum.tile([P, N_BLOCK], F32, tag="bank", name="acc_%d" % i)
-                for i in range(TOKEN_TILES)
-            ]
-            for g0 in range(0, GROUPS, W_GROUPS):
+        for w, n0, width in blocks:
+            groups = W_LOAD_WORDS // width
+            columns = range(0, width, N_BLOCK)
+            accs = {}
+            for c0 in columns:
+                for i in range(TOKEN_TILES):
+                    accs[(i, c0)] = psum.tile(
+                        [P, N_BLOCK], F32, tag="bank", name="acc_%d_%d" % (i, c0)
+                    )
+            for g0 in range(0, GROUPS, groups):
                 w_sb = w_tiles[(w, n0, g0)]
                 for i in range(TOKEN_TILES):
-                    for g in range(g0, g0 + W_GROUPS):
+                    for g in range(g0, g0 + groups):
                         a, b = divmod(g, PLANES_PER_TILE)
-                        nc.tensor.matmul_mx(
-                            out=accs[i][:],
-                            lhsT=x_codes[:, i, g, :].bitcast(FP8X4),
-                            lhsT_scale=x_scales[:, i, g, :],
-                            rhs=w_sb[:, g - g0, :].bitcast(FP8X4),
-                            rhs_scale=planes[4 * b : P, w, a, n0 : n0 + N_BLOCK],
-                            start=(g == 0),
-                            stop=(g == GROUPS - 1),
-                        )
-            for i in range(TOKEN_TILES):
-                rope_relu_store(accs[i], i, w, n0)
+                        for c0 in columns:
+                            nc.tensor.matmul_mx(
+                                out=accs[(i, c0)][:],
+                                lhsT=x_codes[:, i, g, :].bitcast(FP8X4),
+                                lhsT_scale=x_scales[:, i, g, :],
+                                rhs=w_sb[:, g - g0, c0 : c0 + N_BLOCK].bitcast(FP8X4),
+                                rhs_scale=planes[4 * b : P, w, a, n0 + c0 : n0 + c0 + N_BLOCK],
+                                start=(g == 0),
+                                stop=(g == GROUPS - 1),
+                            )
+            for c0 in columns:
+                result = results.tile(
+                    [P, HEADS_PER_BLOCK, TOKEN_TILES, HEAD_DIM],
+                    F32,
+                    name="result_%d_%d" % (w, n0 + c0),
+                )
+                rope_relu([accs[(i, c0)] for i in range(TOKEN_TILES)], result)
+                h0 = (n0 + c0) // HEAD_DIM
+                nc.sync.dma_start(
+                    out=weights[w][2][0, h0 : h0 + HEADS_PER_BLOCK, :, :].rearrange(
+                        "h (p i) d -> p h (i d)", i=TOKEN_TILES
+                    ),
+                    in_=result[:].rearrange("p h i d -> p h (i d)"),
+                )

@@ -27,9 +27,11 @@ PAIRS = HEAD_DIM // 2
 HEADS_PER_BLOCK = N_BLOCK // HEAD_DIM
 ROPE_BASE = 10000.0
 
-X_GROUPS = 8
+X_GROUPS = 4
+CHUNKS = GROUPS // X_GROUPS
 UNIT_GROUPS = 2
 W_LOAD_WORDS = 1024
+TAIL_GROUPS = 6
 PLANES_PER_TILE = 4
 
 ROUND_MAGIC = 12582912.0
@@ -42,19 +44,19 @@ def tile_linearattention_pa_k_kernel(
 ):
     nc = tc.nc
     weights = [(wq_words, wq_scales, out_0), (wk_words, wk_scales, out_1)]
-    blocks = [(0, 0, N_WEIGHT), (1, 0, N_BLOCK), (1, N_BLOCK, N_BLOCK)]
-
     with ExitStack() as ctx:
         keep = ctx.enter_context(tc.tile_pool(name="keep", bufs=1))
-        stage = ctx.enter_context(tc.tile_pool(name="stage", bufs=3))
+        stage = ctx.enter_context(tc.tile_pool(name="stage", bufs=4))
         rope = ctx.enter_context(tc.tile_pool(name="rope", bufs=2))
         results = ctx.enter_context(tc.tile_pool(name="results", bufs=1))
-        psum = ctx.enter_context(tc.psum_pool(name="psum", bufs=8))
+        psum = ctx.enter_context(tc.psum_pool(name="psum", bufs=4))
+        ctx.enter_context(tc.manual_schedule())
 
         planes = keep.tile(
             [P, len(weights), GROUPS // PLANES_PER_TILE, N_WEIGHT], U8, align_bytes=64
         )
-        nc.vector.memset(planes[:].bitcast(I32), 0)
+        for w in range(len(weights)):
+            nc.vector.memset(planes[:, w, :, :].bitcast(I32), 0)
 
         identity = keep.tile([P, P], F32)
         masks.make_identity(nc, identity[:])
@@ -77,9 +79,9 @@ def tile_linearattention_pa_k_kernel(
 
         x_by_tile = x[0].rearrange("(p i) k -> p i k", i=TOKEN_TILES)
 
-        def load_x(i, piece):
-            x_sb = keep.tile([P, X_GROUPS * K_PASS], BF16, name="x_%d_%d" % (i, piece))
-            first = piece * X_GROUPS * K_PASS
+        def load_x(chunk, i):
+            x_sb = keep.tile([P, X_GROUPS * K_PASS], BF16, name="x_%d_%d" % (chunk, i))
+            first = chunk * X_GROUPS * K_PASS
             nc.sync.dma_start(out=x_sb[:], in_=x_by_tile[:, i, first : first + X_GROUPS * K_PASS])
             return x_sb
 
@@ -97,13 +99,20 @@ def tile_linearattention_pa_k_kernel(
             return w_sb
 
         x_tiles = {}
-        for piece in range(GROUPS // X_GROUPS):
-            for i in range(TOKEN_TILES):
-                x_tiles[(i, piece)] = load_x(i, piece)
         w_tiles = {}
-        for w, n0, width in blocks:
-            for g0 in range(0, GROUPS, W_LOAD_WORDS // width):
-                w_tiles[(w, n0, g0)] = load_words(w, n0, width, g0)
+        for chunk in range(CHUNKS):
+            for i in range(TOKEN_TILES):
+                x_tiles[(chunk, i)] = load_x(chunk, i)
+            if chunk > 0:
+                for g in range(X_GROUPS * (chunk - 1), X_GROUPS * chunk):
+                    w_tiles[(0, 0, g)] = load_words(0, 0, N_WEIGHT, g)
+        for g in range(X_GROUPS * (CHUNKS - 1), GROUPS):
+            w_tiles[(0, 0, g)] = load_words(0, 0, N_WEIGHT, g)
+        for g in range(GROUPS - TAIL_GROUPS):
+            w_tiles[(1, 0, g)] = load_words(1, 0, N_WEIGHT, g)
+        for n0 in range(0, N_WEIGHT, N_BLOCK):
+            for g in range(GROUPS - TAIL_GROUPS, GROUPS, W_LOAD_WORDS // N_BLOCK):
+                w_tiles[(1, n0, g)] = load_words(1, n0, N_BLOCK, g)
 
         position = keep.tile([P, TOKEN_TILES], F32)
         nc.vector.tensor_scalar(
@@ -171,8 +180,8 @@ def tile_linearattention_pa_k_kernel(
         x_scales = keep.tile([P, TOKEN_TILES, GROUPS, P], U8, align_bytes=64)
 
         def regroup(i, g0, copy_engine):
-            x_words = x_tiles[(i, g0 // X_GROUPS)][:].bitcast(F32)
-            halves = psum.tile([P, UNIT_GROUPS, 2, P], F32, tag="bank", name="halves")
+            x_words = x_tiles[(g0 // X_GROUPS, i)][:].bitcast(F32)
+            halves = psum.tile([P, UNIT_GROUPS, 2, P], F32, tag="turn", name="halves")
             for gg in range(UNIT_GROUPS):
                 first = (K_PASS // 2) * ((g0 + gg) % X_GROUPS)
                 for u in range(2):
@@ -196,15 +205,14 @@ def tile_linearattention_pa_k_kernel(
                 in_=grouped[:].rearrange("p g s t -> p (g s t)"),
             )
 
-        waiting = None
-        for g0 in range(0, GROUPS, UNIT_GROUPS):
-            for i in range(TOKEN_TILES):
-                copy_engine = nc.vector.tensor_copy if i == 0 else nc.scalar.copy
-                grouped = regroup(i, g0, copy_engine)
-                if waiting is not None:
-                    quantise(*waiting)
-                waiting = (i, g0, grouped)
-        quantise(*waiting)
+        def prepare(chunk):
+            units = []
+            for g0 in range(chunk * X_GROUPS, (chunk + 1) * X_GROUPS, UNIT_GROUPS):
+                for i in range(TOKEN_TILES):
+                    copy_engine = nc.vector.tensor_copy if i == 0 else nc.scalar.copy
+                    units.append((i, g0, regroup(i, g0, copy_engine)))
+            for unit in units:
+                quantise(*unit)
 
         pair_shape = [P, HEADS_PER_BLOCK, PAIRS, 2]
 
@@ -238,41 +246,68 @@ def tile_linearattention_pa_k_kernel(
                     func=ACT.Relu,
                 )
 
-        for w, n0, width in blocks:
-            groups = W_LOAD_WORDS // width
-            columns = range(0, width, N_BLOCK)
+        def multiply(w, i, g, n0, acc):
+            if g < GROUPS - TAIL_GROUPS * w:
+                words = w_tiles[(w, 0, g)][:, 0, n0 : n0 + N_BLOCK]
+            else:
+                first = g - (g - (GROUPS - TAIL_GROUPS)) % (W_LOAD_WORDS // N_BLOCK)
+                words = w_tiles[(w, n0, first)][:, g - first, :]
+            a, b = divmod(g, PLANES_PER_TILE)
+            nc.tensor.matmul_mx(
+                out=acc[:],
+                lhsT=x_codes[:, i, g, :].bitcast(FP8X4),
+                lhsT_scale=x_scales[:, i, g, :],
+                rhs=words.bitcast(FP8X4),
+                rhs_scale=planes[4 * b : P, w, a, n0 : n0 + N_BLOCK],
+                start=(g == 0),
+                stop=(g == GROUPS - 1),
+            )
+
+        def finish(w, n0, banks):
+            result = results.tile(
+                [P, HEADS_PER_BLOCK, TOKEN_TILES, HEAD_DIM], F32, name="result_%d_%d" % (w, n0)
+            )
+            rope_relu(banks, result)
+            h0 = n0 // HEAD_DIM
+            nc.sync.dma_start(
+                out=weights[w][2][0, h0 : h0 + HEADS_PER_BLOCK, :, :].rearrange(
+                    "h (p i) d -> p h (i d)", i=TOKEN_TILES
+                ),
+                in_=result[:].rearrange("p h i d -> p h (i d)"),
+            )
+
+        column_blocks = range(0, N_WEIGHT, N_BLOCK)
+
+        def open_banks(w, tag):
             accs = {}
-            for c0 in columns:
+            for n0 in column_blocks:
                 for i in range(TOKEN_TILES):
-                    accs[(i, c0)] = psum.tile(
-                        [P, N_BLOCK], F32, tag="bank", name="acc_%d_%d" % (i, c0)
+                    accs[(i, n0)] = psum.tile(
+                        [P, N_BLOCK], F32, tag=tag, name="acc_%d_%d_%d" % (w, i, n0)
                     )
-            for g0 in range(0, GROUPS, groups):
-                w_sb = w_tiles[(w, n0, g0)]
+            return accs
+
+        def multiply_group(w, g, accs):
+            for i in range(TOKEN_TILES):
+                for n0 in column_blocks:
+                    multiply(w, i, g, n0, accs[(i, n0)])
+
+        q_accs = open_banks(0, "acc")
+        prepare(0)
+        for chunk in range(CHUNKS):
+            if chunk + 1 < CHUNKS:
+                prepare(chunk + 1)
+            for g in range(chunk * X_GROUPS, (chunk + 1) * X_GROUPS):
+                multiply_group(0, g, q_accs)
+        for n0 in column_blocks:
+            finish(0, n0, [q_accs[(i, n0)] for i in range(TOKEN_TILES)])
+
+        k_accs = open_banks(1, "turn")
+        for g in range(GROUPS - TAIL_GROUPS):
+            multiply_group(1, g, k_accs)
+        for n0 in column_blocks:
+            for g0 in range(GROUPS - TAIL_GROUPS, GROUPS, W_LOAD_WORDS // N_BLOCK):
                 for i in range(TOKEN_TILES):
-                    for g in range(g0, g0 + groups):
-                        a, b = divmod(g, PLANES_PER_TILE)
-                        for c0 in columns:
-                            nc.tensor.matmul_mx(
-                                out=accs[(i, c0)][:],
-                                lhsT=x_codes[:, i, g, :].bitcast(FP8X4),
-                                lhsT_scale=x_scales[:, i, g, :],
-                                rhs=w_sb[:, g - g0, c0 : c0 + N_BLOCK].bitcast(FP8X4),
-                                rhs_scale=planes[4 * b : P, w, a, n0 + c0 : n0 + c0 + N_BLOCK],
-                                start=(g == 0),
-                                stop=(g == GROUPS - 1),
-                            )
-            for c0 in columns:
-                result = results.tile(
-                    [P, HEADS_PER_BLOCK, TOKEN_TILES, HEAD_DIM],
-                    F32,
-                    name="result_%d_%d" % (w, n0 + c0),
-                )
-                rope_relu([accs[(i, c0)] for i in range(TOKEN_TILES)], result)
-                h0 = (n0 + c0) // HEAD_DIM
-                nc.sync.dma_start(
-                    out=weights[w][2][0, h0 : h0 + HEADS_PER_BLOCK, :, :].rearrange(
-                        "h (p i) d -> p h (i d)", i=TOKEN_TILES
-                    ),
-                    in_=result[:].rearrange("p h i d -> p h (i d)"),
-                )
+                    for g in range(g0, g0 + W_LOAD_WORDS // N_BLOCK):
+                        multiply(1, i, g, n0, k_accs[(i, n0)])
+            finish(1, n0, [k_accs[(i, n0)] for i in range(TOKEN_TILES)])

@@ -31,6 +31,7 @@ X_GROUPS = 4
 CHUNKS = GROUPS // X_GROUPS
 UNIT_GROUPS = 2
 W_LOAD_WORDS = 1024
+WARM_UP = 5
 TAIL_GROUPS = 6
 PLANES_PER_TILE = 4
 
@@ -58,6 +59,8 @@ def tile_linearattention_pa_k_kernel(
         for w in range(len(weights)):
             nc.vector.memset(planes[:, w, :, :].bitcast(I32), 0)
 
+        warm = keep.tile([P, N_BLOCK], BF16)
+        nc.gpsimd.memset(warm[:], 0.0)
         identity = keep.tile([P, P], F32)
         masks.make_identity(nc, identity[:])
         position_int = keep.tile([P, TOKEN_TILES], I32)
@@ -205,12 +208,22 @@ def tile_linearattention_pa_k_kernel(
                 in_=grouped[:].rearrange("p g s t -> p (g s t)"),
             )
 
+        warm_bank = psum.tile([P, N_BLOCK], F32, tag="acc", name="warm_bank")
+
+        def warm_up():
+            nc.tensor.matmul(warm_bank[:], lhsT=warm[:, 0:P], rhs=warm[:], start=True, stop=True)
+
+        for n in range(WARM_UP):
+            warm_up()
+
         def prepare(chunk):
             units = []
             for g0 in range(chunk * X_GROUPS, (chunk + 1) * X_GROUPS, UNIT_GROUPS):
                 for i in range(TOKEN_TILES):
                     copy_engine = nc.vector.tensor_copy if i == 0 else nc.scalar.copy
                     units.append((i, g0, regroup(i, g0, copy_engine)))
+                    if chunk < 2:
+                        warm_up()
             for unit in units:
                 quantise(*unit)
 

@@ -22,17 +22,19 @@ D_MODEL = 8192
 GROUPS = D_MODEL // K_PASS
 N_WEIGHT = 1024
 N_BLOCK = 512
+MIN_BLOCK = 256
 HEAD_DIM = 128
 PAIRS = HEAD_DIM // 2
-HEADS_PER_BLOCK = N_BLOCK // HEAD_DIM
 ROPE_BASE = 10000.0
 
 X_GROUPS = 4
 CHUNKS = GROUPS // X_GROUPS
 UNIT_GROUPS = 2
-W_LOAD_WORDS = 1024
+TAIL_LOAD_GROUPS = 2
 WARM_UP = 5
-TAIL_GROUPS = 6
+TAIL_GROUPS = 8
+BLOCKS = (((0, 512), (512, 512)), ((0, 512), (512, 256), (768, 256)))
+LATE_GROUPS = 3
 PLANES_PER_TILE = 4
 
 ROUND_MAGIC = 12582912.0
@@ -88,8 +90,7 @@ def tile_linearattention_pa_k_kernel(
             nc.sync.dma_start(out=x_sb[:], in_=x_by_tile[:, i, first : first + X_GROUPS * K_PASS])
             return x_sb
 
-        def load_words(w, n0, width, g0):
-            groups = W_LOAD_WORDS // width
+        def load_words(w, n0, width, g0, groups):
             w_sb = keep.tile(
                 [P, groups, width], U32, name="w_%d_%d_%d" % (w, n0, g0), align_bytes=64
             )
@@ -99,23 +100,29 @@ def tile_linearattention_pa_k_kernel(
                 .rearrange("g p n t -> p g (n t)")
                 .bitcast(I32),
             )
-            return w_sb
+            for g in range(g0, g0 + groups):
+                for n in range(n0, n0 + width, MIN_BLOCK):
+                    words_at[(w, g, n)] = (w_sb, g - g0, n - n0)
 
         x_tiles = {}
-        w_tiles = {}
+        words_at = {}
         for chunk in range(CHUNKS):
             for i in range(TOKEN_TILES):
                 x_tiles[(chunk, i)] = load_x(chunk, i)
             if chunk > 0:
                 for g in range(X_GROUPS * (chunk - 1), X_GROUPS * chunk):
-                    w_tiles[(0, 0, g)] = load_words(0, 0, N_WEIGHT, g)
+                    load_words(0, 0, N_WEIGHT, g, 1)
         for g in range(X_GROUPS * (CHUNKS - 1), GROUPS):
-            w_tiles[(0, 0, g)] = load_words(0, 0, N_WEIGHT, g)
+            load_words(0, 0, N_WEIGHT, g, 1)
         for g in range(GROUPS - TAIL_GROUPS):
-            w_tiles[(1, 0, g)] = load_words(1, 0, N_WEIGHT, g)
-        for n0 in range(0, N_WEIGHT, N_BLOCK):
-            for g in range(GROUPS - TAIL_GROUPS, GROUPS, W_LOAD_WORDS // N_BLOCK):
-                w_tiles[(1, n0, g)] = load_words(1, n0, N_BLOCK, g)
+            load_words(1, 0, N_WEIGHT, g, 1)
+        tail = [
+            (n0, width, g)
+            for n0, width in BLOCKS[1]
+            for g in range(GROUPS - TAIL_GROUPS, GROUPS, TAIL_LOAD_GROUPS)
+        ]
+        for n0, width, g in tail:
+            load_words(1, n0, width, g, TAIL_LOAD_GROUPS)
 
         position = keep.tile([P, TOKEN_TILES], F32)
         nc.vector.tensor_scalar(
@@ -227,12 +234,11 @@ def tile_linearattention_pa_k_kernel(
             for unit in units:
                 quantise(*unit)
 
-        pair_shape = [P, HEADS_PER_BLOCK, PAIRS, 2]
-
-        def rope_relu(banks, result):
+        def rope_relu(banks, heads, result):
+            pair_shape = [P, heads, PAIRS, 2]
             products = []
             for i in range(TOKEN_TILES):
-                pairs = banks[i][:].rearrange("p (h j e) -> p h j e", h=HEADS_PER_BLOCK, e=2)
+                pairs = banks[i][:].rearrange("p (h j e) -> p h j e", h=heads, e=2)
                 from_even = rope.tile(pair_shape, F32, name="from_even")
                 nc.vector.tensor_tensor(
                     out=from_even[:],
@@ -259,68 +265,67 @@ def tile_linearattention_pa_k_kernel(
                     func=ACT.Relu,
                 )
 
-        def multiply(w, i, g, n0, acc):
-            if g < GROUPS - TAIL_GROUPS * w:
-                words = w_tiles[(w, 0, g)][:, 0, n0 : n0 + N_BLOCK]
-            else:
-                first = g - (g - (GROUPS - TAIL_GROUPS)) % (W_LOAD_WORDS // N_BLOCK)
-                words = w_tiles[(w, n0, first)][:, g - first, :]
+        def multiply(w, g, blocks, accs):
             a, b = divmod(g, PLANES_PER_TILE)
-            nc.tensor.matmul_mx(
-                out=acc[:],
-                lhsT=x_codes[:, i, g, :].bitcast(FP8X4),
-                lhsT_scale=x_scales[:, i, g, :],
-                rhs=words.bitcast(FP8X4),
-                rhs_scale=planes[4 * b : P, w, a, n0 : n0 + N_BLOCK],
-                start=(g == 0),
-                stop=(g == GROUPS - 1),
-            )
+            for i in range(TOKEN_TILES):
+                for n0, width in blocks:
+                    w_sb, g_in, n_in = words_at[(w, g, n0)]
+                    nc.tensor.matmul_mx(
+                        out=accs[(i, n0)][:],
+                        lhsT=x_codes[:, i, g, :].bitcast(FP8X4),
+                        lhsT_scale=x_scales[:, i, g, :],
+                        rhs=w_sb[:, g_in, n_in : n_in + width].bitcast(FP8X4),
+                        rhs_scale=planes[4 * b : P, w, a, n0 : n0 + width],
+                        start=(g == 0),
+                        stop=(g == GROUPS - 1),
+                    )
 
-        def finish(w, n0, banks):
+        def finish(w, n0, width, accs):
+            heads = width // HEAD_DIM
             result = results.tile(
-                [P, HEADS_PER_BLOCK, TOKEN_TILES, HEAD_DIM], F32, name="result_%d_%d" % (w, n0)
+                [P, heads, TOKEN_TILES, HEAD_DIM], F32, name="result_%d_%d" % (w, n0)
             )
-            rope_relu(banks, result)
+            rope_relu([accs[(i, n0)] for i in range(TOKEN_TILES)], heads, result)
             h0 = n0 // HEAD_DIM
             nc.sync.dma_start(
-                out=weights[w][2][0, h0 : h0 + HEADS_PER_BLOCK, :, :].rearrange(
+                out=weights[w][2][0, h0 : h0 + heads, :, :].rearrange(
                     "h (p i) d -> p h (i d)", i=TOKEN_TILES
                 ),
                 in_=result[:].rearrange("p h i d -> p h (i d)"),
             )
 
-        column_blocks = range(0, N_WEIGHT, N_BLOCK)
-
-        def open_banks(w, tag):
-            accs = {}
-            for n0 in column_blocks:
+        def open_banks(w, blocks, tag, accs):
+            for n0, width in blocks:
                 for i in range(TOKEN_TILES):
                     accs[(i, n0)] = psum.tile(
-                        [P, N_BLOCK], F32, tag=tag, name="acc_%d_%d_%d" % (w, i, n0)
+                        [P, width], F32, tag=tag, name="acc_%d_%d_%d" % (w, i, n0)
                     )
-            return accs
 
-        def multiply_group(w, g, accs):
-            for i in range(TOKEN_TILES):
-                for n0 in column_blocks:
-                    multiply(w, i, g, n0, accs[(i, n0)])
-
-        q_accs = open_banks(0, "acc")
+        q_blocks, k_blocks = BLOCKS
+        q_accs = {}
+        open_banks(0, q_blocks, "acc", q_accs)
         prepare(0)
         for chunk in range(CHUNKS):
             if chunk + 1 < CHUNKS:
                 prepare(chunk + 1)
             for g in range(chunk * X_GROUPS, (chunk + 1) * X_GROUPS):
-                multiply_group(0, g, q_accs)
-        for n0 in column_blocks:
-            finish(0, n0, [q_accs[(i, n0)] for i in range(TOKEN_TILES)])
+                multiply(0, g, q_blocks, q_accs)
+        for n0, width in q_blocks:
+            finish(0, n0, width, q_accs)
 
-        k_accs = open_banks(1, "turn")
+        k_accs = {}
+        open_banks(1, k_blocks[:-1], "turn", k_accs)
+        open_banks(1, k_blocks[-1:], "acc", k_accs)
         for g in range(GROUPS - TAIL_GROUPS):
-            multiply_group(1, g, k_accs)
-        for n0 in column_blocks:
-            for g0 in range(GROUPS - TAIL_GROUPS, GROUPS, W_LOAD_WORDS // N_BLOCK):
-                for i in range(TOKEN_TILES):
-                    for g in range(g0, g0 + W_LOAD_WORDS // N_BLOCK):
-                        multiply(1, i, g, n0, k_accs[(i, n0)])
-            finish(1, n0, [k_accs[(i, n0)] for i in range(TOKEN_TILES)])
+            if g < LATE_GROUPS:
+                multiply(1, g, k_blocks[:-1], k_accs)
+            else:
+                if g == LATE_GROUPS:
+                    for late in range(LATE_GROUPS):
+                        multiply(1, late, k_blocks[-1:], k_accs)
+                multiply(1, g, k_blocks, k_accs)
+        for n0, width, g0 in tail:
+            for g in range(g0, g0 + TAIL_LOAD_GROUPS):
+                multiply(1, g, ((n0, width),), k_accs)
+            if g0 + TAIL_LOAD_GROUPS == GROUPS:
+                finish(1, n0, width, k_accs)

@@ -30,6 +30,7 @@ ROPE_BASE = 10000.0
 X_GROUPS = 4
 CHUNKS = GROUPS // X_GROUPS
 UNIT_GROUPS = 2
+EARLY_PLANES = 2
 TAIL_LOAD_GROUPS = 2
 WARM_UP = 5
 TAIL_GROUPS = 8
@@ -50,7 +51,7 @@ def tile_linearattention_pa_k_kernel(
     with ExitStack() as ctx:
         keep = ctx.enter_context(tc.tile_pool(name="keep", bufs=1))
         stage = ctx.enter_context(tc.tile_pool(name="stage", bufs=4))
-        rope = ctx.enter_context(tc.tile_pool(name="rope", bufs=2))
+        rope = ctx.enter_context(tc.tile_pool(name="rope", bufs=3))
         results = ctx.enter_context(tc.tile_pool(name="results", bufs=1))
         psum = ctx.enter_context(tc.psum_pool(name="psum", bufs=4))
         ctx.enter_context(tc.manual_schedule())
@@ -59,7 +60,8 @@ def tile_linearattention_pa_k_kernel(
             [P, len(weights), GROUPS // PLANES_PER_TILE, N_WEIGHT], U8, align_bytes=64
         )
         for w in range(len(weights)):
-            nc.vector.memset(planes[:, w, :, :].bitcast(I32), 0)
+            for a in range(GROUPS // PLANES_PER_TILE):
+                nc.vector.memset(planes[:, w, a, :].bitcast(I32), 0)
 
         warm = keep.tile([P, N_BLOCK], BF16)
         nc.gpsimd.memset(warm[:], 0.0)
@@ -70,17 +72,21 @@ def tile_linearattention_pa_k_kernel(
             position_int[:], pattern=[[1, TOKEN_TILES]], base=0, channel_multiplier=TOKEN_TILES
         )
 
+        def load_scales(queue, view, w, a):
+            for quadrant in range(4):
+                queue.dma_start(
+                    out=planes[32 * quadrant : 32 * quadrant + 16, w, a, :].bitcast(view),
+                    in_=weights[w][1][
+                        PLANES_PER_TILE * a : PLANES_PER_TILE * (a + 1),
+                        4 * quadrant : 4 * quadrant + 4,
+                        :,
+                    ].bitcast(view),
+                )
+
         for w in range(len(weights)):
             for a in range(GROUPS // PLANES_PER_TILE):
-                for quadrant in range(4):
-                    nc.gpsimd.dma_start(
-                        out=planes[32 * quadrant : 32 * quadrant + 16, w, a, :].bitcast(F32),
-                        in_=weights[w][1][
-                            PLANES_PER_TILE * a : PLANES_PER_TILE * (a + 1),
-                            4 * quadrant : 4 * quadrant + 4,
-                            :,
-                        ].bitcast(F32),
-                    )
+                if w > 0 or a >= EARLY_PLANES:
+                    load_scales(nc.gpsimd, F32, w, a)
 
         x_by_tile = x[0].rearrange("(p i) k -> p i k", i=TOKEN_TILES)
 
@@ -109,6 +115,8 @@ def tile_linearattention_pa_k_kernel(
         for chunk in range(CHUNKS):
             for i in range(TOKEN_TILES):
                 x_tiles[(chunk, i)] = load_x(chunk, i)
+            if chunk < EARLY_PLANES:
+                load_scales(nc.sync, I32, 0, chunk)
             if chunk > 0:
                 for g in range(X_GROUPS * (chunk - 1), X_GROUPS * chunk):
                     load_words(0, 0, N_WEIGHT, g, 1)
@@ -234,7 +242,7 @@ def tile_linearattention_pa_k_kernel(
             for unit in units:
                 quantise(*unit)
 
-        def rope_relu(banks, heads, result):
+        def rope_relu(banks, heads, result, adder):
             pair_shape = [P, heads, PAIRS, 2]
             products = []
             for i in range(TOKEN_TILES):
@@ -256,7 +264,7 @@ def tile_linearattention_pa_k_kernel(
                 products.append((from_even, from_odd))
             for i in range(TOKEN_TILES):
                 from_even, from_odd = products[i]
-                nc.vector.tensor_tensor(
+                adder.tensor_tensor(
                     out=from_even[:], in0=from_even[:], in1=from_odd[:], op=ALU.add
                 )
                 nc.scalar.activation(
@@ -280,12 +288,13 @@ def tile_linearattention_pa_k_kernel(
                         stop=(g == GROUPS - 1),
                     )
 
-        def finish(w, n0, width, accs):
+        def finish(w, n0, width, accs, adder):
             heads = width // HEAD_DIM
             result = results.tile(
                 [P, heads, TOKEN_TILES, HEAD_DIM], F32, name="result_%d_%d" % (w, n0)
             )
-            rope_relu([accs[(i, n0)] for i in range(TOKEN_TILES)], heads, result)
+            banks = [accs[(i, n0)] for i in range(TOKEN_TILES)]
+            rope_relu(banks, heads, result, adder)
             h0 = n0 // HEAD_DIM
             nc.sync.dma_start(
                 out=weights[w][2][0, h0 : h0 + heads, :, :].rearrange(
@@ -311,7 +320,7 @@ def tile_linearattention_pa_k_kernel(
             for g in range(chunk * X_GROUPS, (chunk + 1) * X_GROUPS):
                 multiply(0, g, q_blocks, q_accs)
         for n0, width in q_blocks:
-            finish(0, n0, width, q_accs)
+            finish(0, n0, width, q_accs, nc.vector)
 
         k_accs = {}
         open_banks(1, k_blocks[:-1], "turn", k_accs)
@@ -328,4 +337,5 @@ def tile_linearattention_pa_k_kernel(
             for g in range(g0, g0 + TAIL_LOAD_GROUPS):
                 multiply(1, g, ((n0, width),), k_accs)
             if g0 + TAIL_LOAD_GROUPS == GROUPS:
-                finish(1, n0, width, k_accs)
+                last_block = n0 + width == N_WEIGHT
+                finish(1, n0, width, k_accs, nc.vector if last_block else nc.gpsimd)

import math
from contextlib import ExitStack

import concourse.masks as masks
import concourse.mybir as mybir

F32 = mybir.dt.float32
BF16 = mybir.dt.bfloat16
I32 = mybir.dt.int32
U32 = mybir.dt.uint32
U8 = mybir.dt.uint8
FP8X4 = mybir.dt.float8_e4m3fn_x4
ALU = mybir.AluOpType
ACT = mybir.ActivationFunctionType

P = 128
PACK = 4
K_PASS = P * PACK
TOKENS = 256
TOKEN_TILES = TOKENS // P
D_MODEL = 8192
GROUPS = D_MODEL // K_PASS
N_WEIGHT = 1024
N_BLOCK = 512
MIN_BLOCK = 256
HEAD_DIM = 128
PAIRS = HEAD_DIM // 2
ROPE_BASE = 10000.0

X_GROUPS = 4
CHUNKS = GROUPS // X_GROUPS
UNIT_GROUPS = 2
EARLY_PLANES = 2
TAIL_LOAD_GROUPS = 2
WARM_UP = 5
TAIL_GROUPS = 8
BLOCKS = (((0, 512), (512, 512)), ((0, 512), (512, 256), (768, 256)))
LATE_GROUPS = 3
PLANES_PER_TILE = 4

ROUND_MAGIC = 12582912.0

FLOPS = 2 * TOKENS * D_MODEL * 2 * N_WEIGHT


def tile_linearattention_pa_k_kernel(
    tc, x, wq_words, wq_scales, wk_words, wk_scales, out_0, out_1
):
    nc = tc.nc
    weights = [(wq_words, wq_scales, out_0), (wk_words, wk_scales, out_1)]
    with ExitStack() as ctx:
        keep = ctx.enter_context(tc.tile_pool(name="keep", bufs=1))
        stage = ctx.enter_context(tc.tile_pool(name="stage", bufs=4))
        rope = ctx.enter_context(tc.tile_pool(name="rope", bufs=3))
        results = ctx.enter_context(tc.tile_pool(name="results", bufs=1))
        psum = ctx.enter_context(tc.psum_pool(name="psum", bufs=4))
        ctx.enter_context(tc.manual_schedule())

        planes = keep.tile(
            [P, len(weights), GROUPS // PLANES_PER_TILE, N_WEIGHT], U8, align_bytes=64
        )
        for w in range(len(weights)):
            for a in range(GROUPS // PLANES_PER_TILE):
                nc.vector.memset(planes[:, w, a, :].bitcast(I32), 0)

        warm = keep.tile([P, N_BLOCK], BF16)
        nc.gpsimd.memset(warm[:], 0.0)
        identity = keep.tile([P, P], F32)
        masks.make_identity(nc, identity[:])
        position_int = keep.tile([P, TOKEN_TILES], I32)
        nc.gpsimd.iota(
            position_int[:], pattern=[[1, TOKEN_TILES]], base=0, channel_multiplier=TOKEN_TILES
        )

        def load_scales(queue, view, w, a):
            for quadrant in range(4):
                queue.dma_start(
                    out=planes[32 * quadrant : 32 * quadrant + 16, w, a, :].bitcast(view),
                    in_=weights[w][1][
                        PLANES_PER_TILE * a : PLANES_PER_TILE * (a + 1),
                        4 * quadrant : 4 * quadrant + 4,
                        :,
                    ].bitcast(view),
                )

        for w in range(len(weights)):
            for a in range(GROUPS // PLANES_PER_TILE):
                if w > 0 or a >= EARLY_PLANES:
                    load_scales(nc.gpsimd, F32, w, a)

        x_by_tile = x[0].rearrange("(p i) k -> p i k", i=TOKEN_TILES)

        def load_x(chunk, i):
            x_sb = keep.tile([P, X_GROUPS * K_PASS], BF16, name="x_%d_%d" % (chunk, i))
            first = chunk * X_GROUPS * K_PASS
            nc.sync.dma_start(out=x_sb[:], in_=x_by_tile[:, i, first : first + X_GROUPS * K_PASS])
            return x_sb

        def load_words(w, n0, width, g0, groups):
            w_sb = keep.tile(
                [P, groups, width], U32, name="w_%d_%d_%d" % (w, n0, g0), align_bytes=64
            )
            nc.sync.dma_start(
                out=w_sb[:].bitcast(I32),
                in_=weights[w][0][g0 : g0 + groups, :, n0 : n0 + width, :]
                .rearrange("g p n t -> p g (n t)")
                .bitcast(I32),
            )
            for g in range(g0, g0 + groups):
                for n in range(n0, n0 + width, MIN_BLOCK):
                    words_at[(w, g, n)] = (w_sb, g - g0, n - n0)

        x_tiles = {}
        words_at = {}
        for chunk in range(CHUNKS):
            for i in range(TOKEN_TILES):
                x_tiles[(chunk, i)] = load_x(chunk, i)
            if chunk < EARLY_PLANES:
                load_scales(nc.sync, I32, 0, chunk)
            if chunk > 0:
                for g in range(X_GROUPS * (chunk - 1), X_GROUPS * chunk):
                    load_words(0, 0, N_WEIGHT, g, 1)
        for g in range(X_GROUPS * (CHUNKS - 1), GROUPS):
            load_words(0, 0, N_WEIGHT, g, 1)
        for g in range(GROUPS - TAIL_GROUPS):
            load_words(1, 0, N_WEIGHT, g, 1)
        tail = [
            (n0, width, g)
            for n0, width in BLOCKS[1]
            for g in range(GROUPS - TAIL_GROUPS, GROUPS, TAIL_LOAD_GROUPS)
        ]
        for n0, width, g in tail:
            load_words(1, n0, width, g, TAIL_LOAD_GROUPS)

        position = keep.tile([P, TOKEN_TILES], F32)
        nc.vector.tensor_scalar(
            out=position[:],
            in0=position_int[:],
            scalar1=1.0 / (2.0 * math.pi),
            scalar2=None,
            op0=ALU.mult,
        )

        frequency = keep.tile([P, PAIRS], F32)
        nc.vector.memset(frequency[:, 0:1], 1.0)
        width = 1
        while width < PAIRS:
            nc.vector.tensor_scalar(
                out=frequency[:, width : 2 * width],
                in0=frequency[:, 0:width],
                scalar1=ROPE_BASE ** (-width / PAIRS),
                scalar2=None,
                op0=ALU.mult,
            )
            width *= 2

        turns = keep.tile([P, TOKEN_TILES, 2, PAIRS], F32)
        for i in range(TOKEN_TILES):
            for quarter in range(2):
                nc.vector.tensor_scalar(
                    out=turns[:, i, quarter, :],
                    in0=frequency[:],
                    scalar1=position[:, i : i + 1],
                    scalar2=0.25 * quarter,
                    op0=ALU.mult,
                    op1=ALU.add,
                )
        whole_turns = keep.tile([P, TOKEN_TILES, 2, PAIRS], F32)
        nc.vector.tensor_scalar(
            out=whole_turns[:],
            in0=turns[:],
            scalar1=ROUND_MAGIC,
            scalar2=ROUND_MAGIC,
            op0=ALU.add,
            op1=ALU.subtract,
        )
        part_turns = keep.tile([P, TOKEN_TILES, 2, PAIRS], F32)
        nc.vector.tensor_tensor(
            out=part_turns[:], in0=turns[:], in1=whole_turns[:], op=ALU.subtract
        )

        even_coef = keep.tile([P, TOKEN_TILES, PAIRS, 2], F32)
        odd_coef = keep.tile([P, TOKEN_TILES, PAIRS, 2], F32)
        for coef, slot, quarter, sign in (
            (even_coef, 0, 1, 1.0),
            (even_coef, 1, 0, 1.0),
            (odd_coef, 0, 0, -1.0),
            (odd_coef, 1, 1, 1.0),
        ):
            nc.scalar.activation(
                out=coef[:, :, :, slot],
                in_=part_turns[:, :, quarter, :],
                func=ACT.Sin,
                scale=sign * 2.0 * math.pi,
            )

        x_codes = keep.tile([P, TOKEN_TILES, GROUPS, P], U32, align_bytes=64)
        x_scales = keep.tile([P, TOKEN_TILES, GROUPS, P], U8, align_bytes=64)

        def regroup(i, g0, copy_engine):
            x_words = x_tiles[(g0 // X_GROUPS, i)][:].bitcast(F32)
            halves = psum.tile([P, UNIT_GROUPS, 2, P], F32, tag="turn", name="halves")
            for gg in range(UNIT_GROUPS):
                first = (K_PASS // 2) * ((g0 + gg) % X_GROUPS)
                for u in range(2):
                    nc.tensor.transpose(
                        halves[:, gg, u, :],
                        x_words[:, first + u : first + K_PASS // 2 : 2],
                        identity[:],
                    )
            grouped = stage.tile([P, UNIT_GROUPS, P, PACK], BF16, align_bytes=64, name="grouped")
            copy_engine(
                out=grouped[:].bitcast(F32), in_=halves[:].rearrange("p g u s -> p g s u")
            )
            return grouped

        def quantise(i, g0, grouped):
            nc.vector.quantize_mx(
                out=x_codes[:, i, g0 : g0 + UNIT_GROUPS, :]
                .rearrange("p g s -> p (g s)")
                .bitcast(FP8X4),
                scales=x_scales[:, i, g0 : g0 + UNIT_GROUPS, :].rearrange("p g s -> p (g s)"),
                in_=grouped[:].rearrange("p g s t -> p (g s t)"),
            )

        warm_bank = psum.tile([P, N_BLOCK], F32, tag="acc", name="warm_bank")

        def warm_up():
            nc.tensor.matmul(warm_bank[:], lhsT=warm[:, 0:P], rhs=warm[:], start=True, stop=True)

        for n in range(WARM_UP):
            warm_up()

        def prepare(chunk):
            units = []
            for g0 in range(chunk * X_GROUPS, (chunk + 1) * X_GROUPS, UNIT_GROUPS):
                for i in range(TOKEN_TILES):
                    copy_engine = nc.vector.tensor_copy if i == 0 else nc.scalar.copy
                    units.append((i, g0, regroup(i, g0, copy_engine)))
                    if chunk < 2:
                        warm_up()
            for unit in units:
                quantise(*unit)

        def rope_relu(banks, heads, result, adder):
            pair_shape = [P, heads, PAIRS, 2]
            products = []
            for i in range(TOKEN_TILES):
                pairs = banks[i][:].rearrange("p (h j e) -> p h j e", h=heads, e=2)
                from_even = rope.tile(pair_shape, F32, name="from_even")
                nc.vector.tensor_tensor(
                    out=from_even[:],
                    in0=pairs[:, :, :, 0:1].to_broadcast(pair_shape),
                    in1=even_coef[:, i, :, :].unsqueeze(1).to_broadcast(pair_shape),
                    op=ALU.mult,
                )
                from_odd = rope.tile(pair_shape, F32, name="from_odd")
                nc.vector.tensor_tensor(
                    out=from_odd[:],
                    in0=pairs[:, :, :, 1:2].to_broadcast(pair_shape),
                    in1=odd_coef[:, i, :, :].unsqueeze(1).to_broadcast(pair_shape),
                    op=ALU.mult,
                )
                products.append((from_even, from_odd))
            for i in range(TOKEN_TILES):
                from_even, from_odd = products[i]
                adder.tensor_tensor(
                    out=from_even[:], in0=from_even[:], in1=from_odd[:], op=ALU.add
                )
                nc.scalar.activation(
                    out=result[:, :, i, :],
                    in_=from_even[:].rearrange("p h j e -> p h (j e)"),
                    func=ACT.Relu,
                )

        def multiply(w, g, blocks, accs):
            a, b = divmod(g, PLANES_PER_TILE)
            for i in range(TOKEN_TILES):
                for n0, width in blocks:
                    w_sb, g_in, n_in = words_at[(w, g, n0)]
                    nc.tensor.matmul_mx(
                        out=accs[(i, n0)][:],
                        lhsT=x_codes[:, i, g, :].bitcast(FP8X4),
                        lhsT_scale=x_scales[:, i, g, :],
                        rhs=w_sb[:, g_in, n_in : n_in + width].bitcast(FP8X4),
                        rhs_scale=planes[4 * b : P, w, a, n0 : n0 + width],
                        start=(g == 0),
                        stop=(g == GROUPS - 1),
                    )

        def finish(w, n0, width, accs, adder):
            heads = width // HEAD_DIM
            result = results.tile(
                [P, heads, TOKEN_TILES, HEAD_DIM], F32, name="result_%d_%d" % (w, n0)
            )
            banks = [accs[(i, n0)] for i in range(TOKEN_TILES)]
            rope_relu(banks, heads, result, adder)
            h0 = n0 // HEAD_DIM
            nc.sync.dma_start(
                out=weights[w][2][0, h0 : h0 + heads, :, :].rearrange(
                    "h (p i) d -> p h (i d)", i=TOKEN_TILES
                ),
                in_=result[:].rearrange("p h i d -> p h (i d)"),
            )

        def open_banks(w, blocks, tag, accs):
            for n0, width in blocks:
                for i in range(TOKEN_TILES):
                    accs[(i, n0)] = psum.tile(
                        [P, width], F32, tag=tag, name="acc_%d_%d_%d" % (w, i, n0)
                    )

        q_blocks, k_blocks = BLOCKS
        q_accs = {}
        open_banks(0, q_blocks, "acc", q_accs)
        prepare(0)
        for chunk in range(CHUNKS):
            if chunk + 1 < CHUNKS:
                prepare(chunk + 1)
            for g in range(chunk * X_GROUPS, (chunk + 1) * X_GROUPS):
                multiply(0, g, q_blocks, q_accs)
        for n0, width in q_blocks:
            finish(0, n0, width, q_accs, nc.vector)

        k_accs = {}
        open_banks(1, k_blocks[:-1], "turn", k_accs)
        open_banks(1, k_blocks[-1:], "acc", k_accs)
        for g in range(GROUPS - TAIL_GROUPS):
            if g < LATE_GROUPS:
                multiply(1, g, k_blocks[:-1], k_accs)
            else:
                if g == LATE_GROUPS:
                    for late in range(LATE_GROUPS):
                        multiply(1, late, k_blocks[-1:], k_accs)
                multiply(1, g, k_blocks, k_accs)
        for n0, width, g0 in tail:
            for g in range(g0, g0 + TAIL_LOAD_GROUPS):
                multiply(1, g, ((n0, width),), k_accs)
            if g0 + TAIL_LOAD_GROUPS == GROUPS:
                last_block = n0 + width == N_WEIGHT
                finish(1, n0, width, k_accs, nc.vector if last_block else nc.gpsimd)
